import numpy as np
import ml_dtypes

BF16 = ml_dtypes.bfloat16


def bf(x):
    return np.asarray(x, np.float32).astype(BF16)


def f32(x):
    return np.asarray(x, np.float32)


def f64(x):
    return np.asarray(x).astype(np.float64)


def striped(idx):
    return np.tile(idx.reshape(-1, 16).T, (8, 1))


C, S, N, IN, DEG = 512, 2048, 1024, 256, 24


def setup_inputs():
    x = bf(np.random.standard_normal((IN, N)))
    w_in = bf(np.random.standard_normal((IN, C)) / np.sqrt(IN))
    b_in = f32(0.1 * np.random.standard_normal((C, 1)))
    adj_t = bf(np.random.uniform(size=(N, N)) < DEG / N)
    base = f32(0.25 * np.random.standard_normal((C, S)))
    return {"x": x, "w_in": w_in, "b_in": b_in, "adj_t": adj_t, "base": base, "offs": striped(np.random.permutation(S)[:N])}


def reference(x, w_in, b_in, adj_t, base, offs):
    idx = offs[:16].T.reshape(-1)
    h = f64(w_in).T @ f64(x) + f64(b_in)
    a = f64(adj_t)
    total = h @ a
    r = 1.0 / (a.sum(axis=0, keepdims=True) + 1.0)
    out = f64(base).copy()
    out[:, idx] = total * r
    return out

@@ -1,0 +1,96 @@
+import concourse.mybir as mybir
+
+P = 128
+IN, C, N, S = 256, 512, 1024, 2048
+K_BLOCKS = IN // P
+NODE_BLOCKS = N // P
+CHANNEL_BLOCKS = C // P
+PIECE = 512
+PIECES = N // PIECE
+
+BF16, F32, U16 = mybir.dt.bfloat16, mybir.dt.float32, mybir.dt.uint16
+ADD, MULT = mybir.AluOpType.add, mybir.AluOpType.mult
+
+FLOPS = 2 * IN * C * N + 2 * C * N * N + N * N
+BYTES = 2 * (IN * N + IN * C + N * N + N) + 4 * C + 4 * C * (S - N) + 4 * C * S
+
+
+def tile_allgnn_kernel(tc, x, w_in, b_in, adj_t, base, offs, out):
+    nc = tc.nc
+    with (
+        tc.tile_pool(name="held", bufs=1) as held,
+        tc.tile_pool(name="staging", bufs=3) as staging,
+        tc.psum_pool(name="psum_h", bufs=2) as psum_h,
+        tc.psum_pool(name="psum_deg", bufs=2) as psum_deg,
+        tc.psum_pool(name="psum_total", bufs=4) as psum_total,
+    ):
+        offsets = held.tile([P, N // 16], U16, name="offsets")
+        nc.sync.dma_start(offsets[:], offs)
+
+        x_blocks = [held.tile([P, N], BF16, name=f"x{kb}") for kb in range(K_BLOCKS)]
+        w_blocks = [held.tile([P, C], BF16, name=f"w{kb}") for kb in range(K_BLOCKS)]
+        for kb in range(K_BLOCKS):
+            nc.sync.dma_start(x_blocks[kb][:], x[kb * P : (kb + 1) * P, :])
+            nc.sync.dma_start(w_blocks[kb][:], w_in[kb * P : (kb + 1) * P, :])
+
+        bias_rows = held.tile([P, C], F32, name="bias_rows")
+        nc.sync.dma_start(bias_rows[:], b_in.rearrange("c one -> (c one)").partition_broadcast(P))
+
+        adj_blocks = [held.tile([P, N], BF16, name=f"adj{ib}") for ib in range(NODE_BLOCKS)]
+        for ib in range(NODE_BLOCKS):
+            nc.sync.dma_start(adj_blocks[ib][:], adj_t[ib * P : (ib + 1) * P, :])
+
+        windows = [held.tile([P, S], F32, name=f"window{cb}") for cb in range(CHANNEL_BLOCKS)]
+        for cb in range(CHANNEL_BLOCKS):
+            nc.sync.dma_start(windows[cb][:], base[cb * P : (cb + 1) * P, :])
+
+        ones = held.tile([P, P], BF16, name="ones")
+        nc.gpsimd.memset(ones[:], 1.0)
+
+        h_t = [held.tile([P, C], BF16, name=f"h_t{ib}") for ib in range(NODE_BLOCKS)]
+        for ib in range(NODE_BLOCKS):
+            projected = psum_h.tile([P, C], F32, name="projected")
+            for kb in range(K_BLOCKS):
+                nc.tensor.matmul(
+                    projected[:],
+                    x_blocks[kb][:, ib * P : (ib + 1) * P],
+                    w_blocks[kb][:],
+                    start=(kb == 0),
+                    stop=(kb == K_BLOCKS - 1),
+                )
+            nc.vector.tensor_tensor(h_t[ib][:], projected[:], bias_rows[:], ADD)
+
+        r_pieces = [held.tile([P, PIECE], F32, name=f"r{piece}") for piece in range(PIECES)]
+        for piece in range(PIECES):
+            columns = slice(piece * PIECE, (piece + 1) * PIECE)
+            degree = psum_deg.tile([P, PIECE], F32, name="degree")
+            for ib in range(NODE_BLOCKS):
+                nc.tensor.matmul(
+                    degree[:],
+                    ones[:],
+                    adj_blocks[ib][:, columns],
+                    start=(ib == 0),
+                    stop=(ib == NODE_BLOCKS - 1),
+                )
+            nc.vector.tensor_scalar_add(r_pieces[piece][:], degree[:], 1.0)
+            nc.vector.reciprocal(r_pieces[piece][:], r_pieces[piece][:])
+
+        for cb in range(CHANNEL_BLOCKS):
+            for piece in range(PIECES):
+                columns = slice(piece * PIECE, (piece + 1) * PIECE)
+                total = psum_total.tile([P, PIECE], F32, name="total")
+                for ib in range(NODE_BLOCKS):
+                    nc.tensor.matmul(
+                        total[:],
+                        h_t[ib][:, cb * P : (cb + 1) * P],
+                        adj_blocks[ib][:, columns],
+                        start=(ib == 0),
+                        stop=(ib == NODE_BLOCKS - 1),
+                    )
+                staged = staging.tile([P, PIECE], F32, name="staged")
+                nc.scalar.copy(staged[:], total[:])
+                piece_offsets = offsets[:, piece * (PIECE // 16) : (piece + 1) * (PIECE // 16)]
+                nc.vector.tensor_tensor(
+                    windows[cb][:].indirect(piece_offsets), staged[:], r_pieces[piece][:], MULT
+                )
+            nc.sync.dma_start(out[cb * P : (cb + 1) * P, :], windows[cb][:])

@@ -1,4 +1,5 @@
 import concourse.mybir as mybir
+from concourse.masks import make_identity
 
 P = 128
 IN, C, N, S = 256, 512, 1024, 2048
@@ -21,7 +22,7 @@ def tile_allgnn_kernel(tc, x, w_in, b_in, adj_t, base, offs, out):
         tc.tile_pool(name="held", bufs=1) as held,
         tc.tile_pool(name="staging", bufs=3) as staging,
         tc.psum_pool(name="psum_h", bufs=2) as psum_h,
-        tc.psum_pool(name="psum_deg", bufs=2) as psum_deg,
+        tc.psum_pool(name="psum_r", bufs=1) as psum_r,
         tc.psum_pool(name="psum_total", bufs=4) as psum_total,
     ):
         offsets = held.tile([P, N // 16], U16, name="offsets")
@@ -44,8 +45,10 @@ def tile_allgnn_kernel(tc, x, w_in, b_in, adj_t, base, offs, out):
         for cb in range(CHANNEL_BLOCKS):
             nc.sync.dma_start(windows[cb][:], base[cb * P : (cb + 1) * P, :])
 
-        ones = held.tile([P, P], BF16, name="ones")
-        nc.gpsimd.memset(ones[:], 1.0)
+        ones_column = held.tile([P, 1], BF16, name="ones_column")
+        nc.gpsimd.memset(ones_column[:], 1.0)
+        identity = held.tile([P, P], F32, name="identity")
+        make_identity(nc, identity[:])
 
         h_t = [held.tile([P, C], BF16, name=f"h_t{ib}") for ib in range(NODE_BLOCKS)]
         for ib in range(NODE_BLOCKS):
@@ -60,20 +63,31 @@ def tile_allgnn_kernel(tc, x, w_in, b_in, adj_t, base, offs, out):
                 )
             nc.vector.tensor_tensor(h_t[ib][:], projected[:], bias_rows[:], ADD)
 
-        r_pieces = [held.tile([P, PIECE], F32, name=f"r{piece}") for piece in range(PIECES)]
-        for piece in range(PIECES):
-            columns = slice(piece * PIECE, (piece + 1) * PIECE)
-            degree = psum_deg.tile([P, PIECE], F32, name="degree")
+        degree_columns = psum_r.tile([P, NODE_BLOCKS], F32, name="degree_columns")
+        for jb in range(NODE_BLOCKS):
             for ib in range(NODE_BLOCKS):
                 nc.tensor.matmul(
-                    degree[:],
-                    ones[:],
-                    adj_blocks[ib][:, columns],
+                    degree_columns[:, jb : jb + 1],
+                    adj_blocks[ib][:, jb * P : (jb + 1) * P],
+                    ones_column[:],
                     start=(ib == 0),
                     stop=(ib == NODE_BLOCKS - 1),
                 )
-            nc.vector.tensor_scalar_add(r_pieces[piece][:], degree[:], 1.0)
-            nc.vector.reciprocal(r_pieces[piece][:], r_pieces[piece][:])
+        r_columns = held.tile([P, NODE_BLOCKS], F32, name="r_columns")
+        nc.vector.tensor_scalar_add(r_columns[:], degree_columns[:], 1.0)
+        nc.vector.reciprocal(r_columns[:], r_columns[:])
+
+        r_pieces = [held.tile([P, PIECE], F32, name=f"r{piece}") for piece in range(PIECES)]
+        for piece in range(PIECES):
+            r_rows = psum_r.tile([P, PIECE], F32, name="r_rows")
+            for quarter in range(PIECE // P):
+                jb = piece * (PIECE // P) + quarter
+                nc.tensor.transpose(
+                    r_rows[:, quarter * P : (quarter + 1) * P],
+                    r_columns[:, jb : jb + 1].to_broadcast([P, P]),
+                    identity[:],
+                )
+            nc.scalar.copy(r_pieces[piece][:], r_rows[:])
 
         for cb in range(CHANNEL_BLOCKS):
             for piece in range(PIECES):

@@ -8,9 +8,12 @@ NODE_BLOCKS = N // P
 CHANNEL_BLOCKS = C // P
 PIECE = 512
 PIECES = N // PIECE
+BLOCKS_A_PIECE = PIECE // P
+PIECEWISE_BLOCKS = 2
 
 BF16, F32, U16 = mybir.dt.bfloat16, mybir.dt.float32, mybir.dt.uint16
 ADD, MULT = mybir.AluOpType.add, mybir.AluOpType.mult
+IDENTITY = mybir.ActivationFunctionType.Identity
 
 FLOPS = 2 * IN * C * N + 2 * C * N * N + N * N
 BYTES = 2 * (IN * N + IN * C + N * N + N) + 4 * C + 4 * C * (S - N) + 4 * C * S
@@ -20,91 +23,128 @@ def tile_allgnn_kernel(tc, x, w_in, b_in, adj_t, base, offs, out):
     nc = tc.nc
     with (
         tc.tile_pool(name="held", bufs=1) as held,
+        tc.tile_pool(name="h_pool", bufs=2) as h_pool,
         tc.tile_pool(name="staging", bufs=3) as staging,
         tc.psum_pool(name="psum_h", bufs=2) as psum_h,
         tc.psum_pool(name="psum_r", bufs=1) as psum_r,
-        tc.psum_pool(name="psum_total", bufs=4) as psum_total,
+        tc.psum_pool(name="psum_total", bufs=2) as psum_total,
     ):
         offsets = held.tile([P, N // 16], U16, name="offsets")
         nc.sync.dma_start(offsets[:], offs)
 
-        x_blocks = [held.tile([P, N], BF16, name=f"x{kb}") for kb in range(K_BLOCKS)]
         w_blocks = [held.tile([P, C], BF16, name=f"w{kb}") for kb in range(K_BLOCKS)]
+        x_blocks = [held.tile([P, N], BF16, name=f"x{kb}") for kb in range(K_BLOCKS)]
         for kb in range(K_BLOCKS):
-            nc.sync.dma_start(x_blocks[kb][:], x[kb * P : (kb + 1) * P, :])
             nc.sync.dma_start(w_blocks[kb][:], w_in[kb * P : (kb + 1) * P, :])
-
-        bias_rows = held.tile([P, C], F32, name="bias_rows")
-        nc.sync.dma_start(bias_rows[:], b_in.rearrange("c one -> (c one)").partition_broadcast(P))
-
+            nc.sync.dma_start(x_blocks[kb][:], x[kb * P : (kb + 1) * P, :])
         adj_blocks = [held.tile([P, N], BF16, name=f"adj{ib}") for ib in range(NODE_BLOCKS)]
         for ib in range(NODE_BLOCKS):
             nc.sync.dma_start(adj_blocks[ib][:], adj_t[ib * P : (ib + 1) * P, :])
-
         windows = [held.tile([P, S], F32, name=f"window{cb}") for cb in range(CHANNEL_BLOCKS)]
         for cb in range(CHANNEL_BLOCKS):
             nc.sync.dma_start(windows[cb][:], base[cb * P : (cb + 1) * P, :])
 
+        bias_columns = held.tile([P, CHANNEL_BLOCKS], F32, name="bias_columns")
+        with nc.allow_non_contiguous_dma(reason="512 numbers, one to a partition and column"):
+            nc.scalar.dma_start(bias_columns[:], b_in.rearrange("(cb p) one -> p (cb one)", p=P))
+
         ones_column = held.tile([P, 1], BF16, name="ones_column")
         nc.gpsimd.memset(ones_column[:], 1.0)
-        identity = held.tile([P, P], F32, name="identity")
-        make_identity(nc, identity[:])
+        identity_bf16 = held.tile([P, P], BF16, name="identity_bf16")
+        make_identity(nc, identity_bf16[:])
+        identity_f32 = held.tile([P, P], F32, name="identity_f32")
+        make_identity(nc, identity_f32[:])
 
-        h_t = [held.tile([P, C], BF16, name=f"h_t{ib}") for ib in range(NODE_BLOCKS)]
-        for ib in range(NODE_BLOCKS):
-            projected = psum_h.tile([P, C], F32, name="projected")
-            for kb in range(K_BLOCKS):
-                nc.tensor.matmul(
-                    projected[:],
-                    x_blocks[kb][:, ib * P : (ib + 1) * P],
-                    w_blocks[kb][:],
-                    start=(kb == 0),
-                    stop=(kb == K_BLOCKS - 1),
-                )
-            nc.vector.tensor_tensor(h_t[ib][:], projected[:], bias_rows[:], ADD)
+        adj_sum = held.tile([P, N], BF16, name="adj_sum")
+        nc.vector.tensor_tensor(adj_sum[:], adj_blocks[0][:], adj_blocks[1][:], ADD)
+        for ib in range(2, NODE_BLOCKS):
+            nc.vector.tensor_tensor(adj_sum[:], adj_sum[:], adj_blocks[ib][:], ADD)
 
-        degree_columns = psum_r.tile([P, NODE_BLOCKS], F32, name="degree_columns")
-        for jb in range(NODE_BLOCKS):
+        h_tiles = {}
+        h_flipped = [held.tile([P, NODE_BLOCKS, P], BF16, name=f"h_flipped{cb}") for cb in range(CHANNEL_BLOCKS)]
+        r_columns = held.tile([P, NODE_BLOCKS], F32, name="r_columns")
+        r_rows = held.tile([P, N], F32, name="r_rows")
+
+        def project(cb):
+            h = h_pool.tile([P, N], BF16, name="h")
+            h_tiles[cb] = h
+            for piece in range(PIECES):
+                columns = slice(piece * PIECE, (piece + 1) * PIECE)
+                projected = psum_h.tile([P, PIECE], F32, name="projected")
+                for kb in range(K_BLOCKS):
+                    nc.tensor.matmul(
+                        projected[:],
+                        w_blocks[kb][:, cb * P : (cb + 1) * P],
+                        x_blocks[kb][:, columns],
+                        start=(kb == 0),
+                        stop=(kb == K_BLOCKS - 1),
+                    )
+                nc.scalar.activation(h[:, columns], projected[:], IDENTITY, bias=bias_columns[:, cb : cb + 1])
+
+        def flip(cb):
+            for piece in range(PIECES):
+                blocks = slice(piece * BLOCKS_A_PIECE, (piece + 1) * BLOCKS_A_PIECE)
+                flipped = psum_h.tile([P, BLOCKS_A_PIECE, P], BF16, name="flipped")
+                for quarter in range(BLOCKS_A_PIECE):
+                    ib = piece * BLOCKS_A_PIECE + quarter
+                    nc.tensor.transpose(flipped[:, quarter, :], h_tiles[cb][:, ib * P : (ib + 1) * P], identity_bf16[:])
+                nc.scalar.copy(h_flipped[cb][:, blocks, :], flipped[:])
+
+        def neighbour_sums(cb, piece, staged):
+            total = psum_total.tile([P, PIECE], F32, name="total")
             for ib in range(NODE_BLOCKS):
                 nc.tensor.matmul(
-                    degree_columns[:, jb : jb + 1],
-                    adj_blocks[ib][:, jb * P : (jb + 1) * P],
-                    ones_column[:],
+                    total[:],
+                    h_flipped[cb][:, ib, :],
+                    adj_blocks[ib][:, piece * PIECE : (piece + 1) * PIECE],
                     start=(ib == 0),
                     stop=(ib == NODE_BLOCKS - 1),
                 )
-        r_columns = held.tile([P, NODE_BLOCKS], F32, name="r_columns")
-        nc.vector.tensor_scalar_add(r_columns[:], degree_columns[:], 1.0)
-        nc.vector.reciprocal(r_columns[:], r_columns[:])
+            nc.scalar.copy(staged[:, piece * PIECE : (piece + 1) * PIECE], total[:])
 
-        r_pieces = [held.tile([P, PIECE], F32, name=f"r{piece}") for piece in range(PIECES)]
-        for piece in range(PIECES):
-            r_rows = psum_r.tile([P, PIECE], F32, name="r_rows")
-            for quarter in range(PIECE // P):
-                jb = piece * (PIECE // P) + quarter
+        def reciprocal_columns():
+            degree_columns = psum_r.tile([P, NODE_BLOCKS], F32, name="degree_columns")
+            for jb in range(NODE_BLOCKS):
+                nc.tensor.matmul(degree_columns[:, jb : jb + 1], adj_sum[:, jb * P : (jb + 1) * P], ones_column[:])
+            nc.vector.tensor_scalar_add(r_columns[:], degree_columns[:], 1.0)
+            nc.vector.reciprocal(r_columns[:], r_columns[:])
+
+        def spread_r(piece):
+            turned = psum_r.tile([P, PIECE], F32, name="turned")
+            for quarter in range(BLOCKS_A_PIECE):
+                jb = piece * BLOCKS_A_PIECE + quarter
                 nc.tensor.transpose(
-                    r_rows[:, quarter * P : (quarter + 1) * P],
+                    turned[:, quarter * P : (quarter + 1) * P],
                     r_columns[:, jb : jb + 1].to_broadcast([P, P]),
-                    identity[:],
+                    identity_f32[:],
                 )
-            nc.scalar.copy(r_pieces[piece][:], r_rows[:])
+            nc.scalar.copy(r_rows[:, piece * PIECE : (piece + 1) * PIECE], turned[:])
 
-        for cb in range(CHANNEL_BLOCKS):
-            for piece in range(PIECES):
-                columns = slice(piece * PIECE, (piece + 1) * PIECE)
-                total = psum_total.tile([P, PIECE], F32, name="total")
-                for ib in range(NODE_BLOCKS):
-                    nc.tensor.matmul(
-                        total[:],
-                        h_t[ib][:, cb * P : (cb + 1) * P],
-                        adj_blocks[ib][:, columns],
-                        start=(ib == 0),
-                        stop=(ib == NODE_BLOCKS - 1),
-                    )
-                staged = staging.tile([P, PIECE], F32, name="staged")
-                nc.scalar.copy(staged[:], total[:])
-                piece_offsets = offsets[:, piece * (PIECE // 16) : (piece + 1) * (PIECE // 16)]
-                nc.vector.tensor_tensor(
-                    windows[cb][:].indirect(piece_offsets), staged[:], r_pieces[piece][:], MULT
-                )
+        def place(cb, staged, first_piece, pieces):
+            columns = slice(first_piece * PIECE, (first_piece + pieces) * PIECE)
+            entries = offsets[:, first_piece * (PIECE // 16) : (first_piece + pieces) * (PIECE // 16)]
+            nc.vector.tensor_tensor(windows[cb][:].indirect(entries), staged[:, columns], r_rows[:, columns], MULT)
+
+        def store(cb):
             nc.sync.dma_start(out[cb * P : (cb + 1) * P, :], windows[cb][:])
+
+        project(0)
+        flip(0)
+        for cb in range(CHANNEL_BLOCKS):
+            staged = staging.tile([P, N], F32, name="staged")
+            for piece in range(PIECES):
+                neighbour_sums(cb, piece, staged)
+                if cb == 0:
+                    if piece == 0:
+                        reciprocal_columns()
+                        project(1)
+                    spread_r(piece)
+                if cb < PIECEWISE_BLOCKS:
+                    place(cb, staged, piece, 1)
+            if cb >= PIECEWISE_BLOCKS:
+                place(cb, staged, 0, PIECES)
+            store(cb)
+            if cb + 1 < CHANNEL_BLOCKS:
+                flip(cb + 1)
+            if cb + 2 < CHANNEL_BLOCKS:
+                project(cb + 2)

@@ -9,7 +9,6 @@ CHANNEL_BLOCKS = C // P
 PIECE = 512
 PIECES = N // PIECE
 BLOCKS_A_PIECE = PIECE // P
-PIECEWISE_BLOCKS = 2
 
 BF16, F32, U16 = mybir.dt.bfloat16, mybir.dt.float32, mybir.dt.uint16
 ADD, MULT = mybir.AluOpType.add, mybir.AluOpType.mult
@@ -24,7 +23,7 @@ def tile_allgnn_kernel(tc, x, w_in, b_in, adj_t, base, offs, out):
     with (
         tc.tile_pool(name="held", bufs=1) as held,
         tc.tile_pool(name="h_pool", bufs=2) as h_pool,
-        tc.tile_pool(name="staging", bufs=3) as staging,
+        tc.tile_pool(name="staging", bufs=4) as staging,
         tc.psum_pool(name="psum_h", bufs=2) as psum_h,
         tc.psum_pool(name="psum_r", bufs=1) as psum_r,
         tc.psum_pool(name="psum_total", bufs=2) as psum_total,
@@ -90,7 +89,7 @@ def tile_allgnn_kernel(tc, x, w_in, b_in, adj_t, base, offs, out):
                     nc.tensor.transpose(flipped[:, quarter, :], h_tiles[cb][:, ib * P : (ib + 1) * P], identity_bf16[:])
                 nc.scalar.copy(h_flipped[cb][:, blocks, :], flipped[:])
 
-        def neighbour_sums(cb, piece, staged):
+        def neighbour_sums(cb, piece):
             total = psum_total.tile([P, PIECE], F32, name="total")
             for ib in range(NODE_BLOCKS):
                 nc.tensor.matmul(
@@ -100,7 +99,9 @@ def tile_allgnn_kernel(tc, x, w_in, b_in, adj_t, base, offs, out):
                     start=(ib == 0),
                     stop=(ib == NODE_BLOCKS - 1),
                 )
-            nc.scalar.copy(staged[:, piece * PIECE : (piece + 1) * PIECE], total[:])
+            staged = staging.tile([P, PIECE], F32, name="staged")
+            nc.scalar.copy(staged[:], total[:])
+            return staged
 
         def reciprocal_columns():
             degree_columns = psum_r.tile([P, NODE_BLOCKS], F32, name="degree_columns")
@@ -120,10 +121,10 @@ def tile_allgnn_kernel(tc, x, w_in, b_in, adj_t, base, offs, out):
                 )
             nc.scalar.copy(r_rows[:, piece * PIECE : (piece + 1) * PIECE], turned[:])
 
-        def place(cb, staged, first_piece, pieces):
-            columns = slice(first_piece * PIECE, (first_piece + pieces) * PIECE)
-            entries = offsets[:, first_piece * (PIECE // 16) : (first_piece + pieces) * (PIECE // 16)]
-            nc.vector.tensor_tensor(windows[cb][:].indirect(entries), staged[:, columns], r_rows[:, columns], MULT)
+        def place(cb, piece, staged):
+            entries = offsets[:, piece * (PIECE // 16) : (piece + 1) * (PIECE // 16)]
+            r_piece = r_rows[:, piece * PIECE : (piece + 1) * PIECE]
+            nc.vector.tensor_tensor(windows[cb][:].indirect(entries), staged[:], r_piece, MULT)
 
         def store(cb):
             nc.sync.dma_start(out[cb * P : (cb + 1) * P, :], windows[cb][:])
@@ -131,18 +132,14 @@ def tile_allgnn_kernel(tc, x, w_in, b_in, adj_t, base, offs, out):
         project(0)
         flip(0)
         for cb in range(CHANNEL_BLOCKS):
-            staged = staging.tile([P, N], F32, name="staged")
             for piece in range(PIECES):
-                neighbour_sums(cb, piece, staged)
+                staged = neighbour_sums(cb, piece)
                 if cb == 0:
                     if piece == 0:
                         reciprocal_columns()
                         project(1)
                     spread_r(piece)
-                if cb < PIECEWISE_BLOCKS:
-                    place(cb, staged, piece, 1)
-            if cb >= PIECEWISE_BLOCKS:
-                place(cb, staged, 0, PIECES)
+                place(cb, piece, staged)
             store(cb)
             if cb + 1 < CHANNEL_BLOCKS:
                 flip(cb + 1)

@@ -9,6 +9,7 @@ CHANNEL_BLOCKS = C // P
 PIECE = 512
 PIECES = N // PIECE
 BLOCKS_A_PIECE = PIECE // P
+PIECEWISE_BLOCKS = 2
 
 BF16, F32, U16 = mybir.dt.bfloat16, mybir.dt.float32, mybir.dt.uint16
 ADD, MULT = mybir.AluOpType.add, mybir.AluOpType.mult
@@ -23,7 +24,7 @@ def tile_allgnn_kernel(tc, x, w_in, b_in, adj_t, base, offs, out):
     with (
         tc.tile_pool(name="held", bufs=1) as held,
         tc.tile_pool(name="h_pool", bufs=2) as h_pool,
-        tc.tile_pool(name="staging", bufs=4) as staging,
+        tc.tile_pool(name="staging", bufs=3) as staging,
         tc.psum_pool(name="psum_h", bufs=2) as psum_h,
         tc.psum_pool(name="psum_r", bufs=1) as psum_r,
         tc.psum_pool(name="psum_total", bufs=2) as psum_total,
@@ -47,8 +48,8 @@ def tile_allgnn_kernel(tc, x, w_in, b_in, adj_t, base, offs, out):
         with nc.allow_non_contiguous_dma(reason="512 numbers, one to a partition and column"):
             nc.scalar.dma_start(bias_columns[:], b_in.rearrange("(cb p) one -> p (cb one)", p=P))
 
-        ones_column = held.tile([P, 1], BF16, name="ones_column")
-        nc.gpsimd.memset(ones_column[:], 1.0)
+        ones = held.tile([P, NODE_BLOCKS], BF16, name="ones")
+        nc.gpsimd.memset(ones[:], 1.0)
         identity_bf16 = held.tile([P, P], BF16, name="identity_bf16")
         make_identity(nc, identity_bf16[:])
         identity_f32 = held.tile([P, P], F32, name="identity_f32")
@@ -59,37 +60,37 @@ def tile_allgnn_kernel(tc, x, w_in, b_in, adj_t, base, offs, out):
         for ib in range(2, NODE_BLOCKS):
             nc.vector.tensor_tensor(adj_sum[:], adj_sum[:], adj_blocks[ib][:], ADD)
 
-        h_tiles = {}
         h_flipped = [held.tile([P, NODE_BLOCKS, P], BF16, name=f"h_flipped{cb}") for cb in range(CHANNEL_BLOCKS)]
         r_columns = held.tile([P, NODE_BLOCKS], F32, name="r_columns")
         r_rows = held.tile([P, N], F32, name="r_rows")
 
         def project(cb):
             h = h_pool.tile([P, N], BF16, name="h")
-            h_tiles[cb] = h
             for piece in range(PIECES):
-                columns = slice(piece * PIECE, (piece + 1) * PIECE)
                 projected = psum_h.tile([P, PIECE], F32, name="projected")
                 for kb in range(K_BLOCKS):
                     nc.tensor.matmul(
                         projected[:],
                         w_blocks[kb][:, cb * P : (cb + 1) * P],
-                        x_blocks[kb][:, columns],
+                        x_blocks[kb][:, piece * PIECE : (piece + 1) * PIECE],
                         start=(kb == 0),
                         stop=(kb == K_BLOCKS - 1),
                     )
-                nc.scalar.activation(h[:, columns], projected[:], IDENTITY, bias=bias_columns[:, cb : cb + 1])
+                nc.scalar.activation(
+                    h[:, piece * PIECE : (piece + 1) * PIECE], projected[:], IDENTITY, bias=bias_columns[:, cb : cb + 1]
+                )
+            return h
 
-        def flip(cb):
+        def flip(cb, h):
             for piece in range(PIECES):
                 blocks = slice(piece * BLOCKS_A_PIECE, (piece + 1) * BLOCKS_A_PIECE)
                 flipped = psum_h.tile([P, BLOCKS_A_PIECE, P], BF16, name="flipped")
                 for quarter in range(BLOCKS_A_PIECE):
                     ib = piece * BLOCKS_A_PIECE + quarter
-                    nc.tensor.transpose(flipped[:, quarter, :], h_tiles[cb][:, ib * P : (ib + 1) * P], identity_bf16[:])
+                    nc.tensor.transpose(flipped[:, quarter, :], h[:, ib * P : (ib + 1) * P], identity_bf16[:])
                 nc.scalar.copy(h_flipped[cb][:, blocks, :], flipped[:])
 
-        def neighbour_sums(cb, piece):
+        def neighbour_sums(cb, piece, staged):
             total = psum_total.tile([P, PIECE], F32, name="total")
             for ib in range(NODE_BLOCKS):
                 nc.tensor.matmul(
@@ -99,16 +100,20 @@ def tile_allgnn_kernel(tc, x, w_in, b_in, adj_t, base, offs, out):
                     start=(ib == 0),
                     stop=(ib == NODE_BLOCKS - 1),
                 )
-            staged = staging.tile([P, PIECE], F32, name="staged")
-            nc.scalar.copy(staged[:], total[:])
-            return staged
+            nc.scalar.copy(staged[:, piece * PIECE : (piece + 1) * PIECE], total[:])
 
         def reciprocal_columns():
-            degree_columns = psum_r.tile([P, NODE_BLOCKS], F32, name="degree_columns")
+            degree_plus_one = psum_r.tile([P, NODE_BLOCKS], F32, name="degree_plus_one")
+            nc.tensor.matmul(degree_plus_one[:], identity_bf16[:], ones[:], start=True, stop=False)
             for jb in range(NODE_BLOCKS):
-                nc.tensor.matmul(degree_columns[:, jb : jb + 1], adj_sum[:, jb * P : (jb + 1) * P], ones_column[:])
-            nc.vector.tensor_scalar_add(r_columns[:], degree_columns[:], 1.0)
-            nc.vector.reciprocal(r_columns[:], r_columns[:])
+                nc.tensor.matmul(
+                    degree_plus_one[:, jb : jb + 1],
+                    adj_sum[:, jb * P : (jb + 1) * P],
+                    ones[:, 0:1],
+                    start=False,
+                    stop=(jb == NODE_BLOCKS - 1),
+                )
+            nc.vector.reciprocal(r_columns[:], degree_plus_one[:])
 
         def spread_r(piece):
             turned = psum_r.tile([P, PIECE], F32, name="turned")
@@ -121,27 +126,25 @@ def tile_allgnn_kernel(tc, x, w_in, b_in, adj_t, base, offs, out):
                 )
             nc.scalar.copy(r_rows[:, piece * PIECE : (piece + 1) * PIECE], turned[:])
 
-        def place(cb, piece, staged):
-            entries = offsets[:, piece * (PIECE // 16) : (piece + 1) * (PIECE // 16)]
-            r_piece = r_rows[:, piece * PIECE : (piece + 1) * PIECE]
-            nc.vector.tensor_tensor(windows[cb][:].indirect(entries), staged[:], r_piece, MULT)
+        def place(cb, staged, first_piece, pieces):
+            columns = slice(first_piece * PIECE, (first_piece + pieces) * PIECE)
+            entries = offsets[:, first_piece * (PIECE // 16) : (first_piece + pieces) * (PIECE // 16)]
+            nc.vector.tensor_tensor(windows[cb][:].indirect(entries), staged[:, columns], r_rows[:, columns], MULT)
 
-        def store(cb):
-            nc.sync.dma_start(out[cb * P : (cb + 1) * P, :], windows[cb][:])
-
-        project(0)
-        flip(0)
+        h = project(0)
         for cb in range(CHANNEL_BLOCKS):
+            flip(cb, h)
+            if cb + 1 < CHANNEL_BLOCKS:
+                h = project(cb + 1)
+            staged = staging.tile([P, N], F32, name="staged")
             for piece in range(PIECES):
-                staged = neighbour_sums(cb, piece)
+                neighbour_sums(cb, piece, staged)
                 if cb == 0:
                     if piece == 0:
                         reciprocal_columns()
-                        project(1)
                     spread_r(piece)
-                place(cb, piece, staged)
-            store(cb)
-            if cb + 1 < CHANNEL_BLOCKS:
-                flip(cb + 1)
-            if cb + 2 < CHANNEL_BLOCKS:
-                project(cb + 2)
+                if cb < PIECEWISE_BLOCKS:
+                    place(cb, staged, piece, 1)
+            if cb >= PIECEWISE_BLOCKS:
+                place(cb, staged, 0, PIECES)
+            nc.sync.dma_start(out[cb * P : (cb + 1) * P, :], windows[cb][:])

@@ -12,7 +12,7 @@ BLOCKS_A_PIECE = PIECE // P
 PIECEWISE_BLOCKS = 2
 
 BF16, F32, U16 = mybir.dt.bfloat16, mybir.dt.float32, mybir.dt.uint16
-ADD, MULT = mybir.AluOpType.add, mybir.AluOpType.mult
+MULT = mybir.AluOpType.mult
 IDENTITY = mybir.ActivationFunctionType.Identity
 
 FLOPS = 2 * IN * C * N + 2 * C * N * N + N * N
@@ -55,14 +55,11 @@ def tile_allgnn_kernel(tc, x, w_in, b_in, adj_t, base, offs, out):
         identity_f32 = held.tile([P, P], F32, name="identity_f32")
         make_identity(nc, identity_f32[:])
 
-        adj_sum = held.tile([P, N], BF16, name="adj_sum")
-        nc.vector.tensor_tensor(adj_sum[:], adj_blocks[0][:], adj_blocks[1][:], ADD)
-        for ib in range(2, NODE_BLOCKS):
-            nc.vector.tensor_tensor(adj_sum[:], adj_sum[:], adj_blocks[ib][:], ADD)
-
         h_flipped = [held.tile([P, NODE_BLOCKS, P], BF16, name=f"h_flipped{cb}") for cb in range(CHANNEL_BLOCKS)]
         r_columns = held.tile([P, NODE_BLOCKS], F32, name="r_columns")
         r_rows = held.tile([P, N], F32, name="r_rows")
+
+        BLOCK_EMPTIED_BY_VECTOR = 1
 
         def project(cb):
             h = h_pool.tile([P, N], BF16, name="h")
@@ -76,9 +73,11 @@ def tile_allgnn_kernel(tc, x, w_in, b_in, adj_t, base, offs, out):
                         start=(kb == 0),
                         stop=(kb == K_BLOCKS - 1),
                     )
-                nc.scalar.activation(
-                    h[:, piece * PIECE : (piece + 1) * PIECE], projected[:], IDENTITY, bias=bias_columns[:, cb : cb + 1]
-                )
+                columns = slice(piece * PIECE, (piece + 1) * PIECE)
+                if cb == BLOCK_EMPTIED_BY_VECTOR:
+                    nc.vector.tensor_scalar_add(h[:, columns], projected[:], bias_columns[:, cb : cb + 1])
+                else:
+                    nc.scalar.activation(h[:, columns], projected[:], IDENTITY, bias=bias_columns[:, cb : cb + 1])
             return h
 
         def flip(cb, h):
@@ -88,7 +87,10 @@ def tile_allgnn_kernel(tc, x, w_in, b_in, adj_t, base, offs, out):
                 for quarter in range(BLOCKS_A_PIECE):
                     ib = piece * BLOCKS_A_PIECE + quarter
                     nc.tensor.transpose(flipped[:, quarter, :], h[:, ib * P : (ib + 1) * P], identity_bf16[:])
-                nc.scalar.copy(h_flipped[cb][:, blocks, :], flipped[:])
+                if cb == BLOCK_EMPTIED_BY_VECTOR:
+                    nc.vector.tensor_copy(h_flipped[cb][:, blocks, :], flipped[:])
+                else:
+                    nc.scalar.copy(h_flipped[cb][:, blocks, :], flipped[:])
 
         def neighbour_sums(cb, piece, staged):
             total = psum_total.tile([P, PIECE], F32, name="total")
@@ -105,14 +107,15 @@ def tile_allgnn_kernel(tc, x, w_in, b_in, adj_t, base, offs, out):
         def reciprocal_columns():
             degree_plus_one = psum_r.tile([P, NODE_BLOCKS], F32, name="degree_plus_one")
             nc.tensor.matmul(degree_plus_one[:], identity_bf16[:], ones[:], start=True, stop=False)
-            for jb in range(NODE_BLOCKS):
-                nc.tensor.matmul(
-                    degree_plus_one[:, jb : jb + 1],
-                    adj_sum[:, jb * P : (jb + 1) * P],
-                    ones[:, 0:1],
-                    start=False,
-                    stop=(jb == NODE_BLOCKS - 1),
-                )
+            for ib in range(NODE_BLOCKS):
+                for jb in range(NODE_BLOCKS):
+                    nc.tensor.matmul(
+                        degree_plus_one[:, jb : jb + 1],
+                        adj_blocks[ib][:, jb * P : (jb + 1) * P],
+                        ones[:, 0:1],
+                        start=False,
+                        stop=(ib == NODE_BLOCKS - 1 and jb == NODE_BLOCKS - 1),
+                    )
             nc.vector.reciprocal(r_columns[:], degree_plus_one[:])
 
         def spread_r(piece):
@@ -131,17 +134,19 @@ def tile_allgnn_kernel(tc, x, w_in, b_in, adj_t, base, offs, out):
             entries = offsets[:, first_piece * (PIECE // 16) : (first_piece + pieces) * (PIECE // 16)]
             nc.vector.tensor_tensor(windows[cb][:].indirect(entries), staged[:, columns], r_rows[:, columns], MULT)
 
-        h = project(0)
+        for cb in range(2):
+            flip(cb, project(cb))
         for cb in range(CHANNEL_BLOCKS):
-            flip(cb, h)
-            if cb + 1 < CHANNEL_BLOCKS:
+            if cb >= 2:
+                flip(cb, h)
+            if 1 <= cb < CHANNEL_BLOCKS - 1:
                 h = project(cb + 1)
             staged = staging.tile([P, N], F32, name="staged")
             for piece in range(PIECES):
+                if cb == 0 and piece == 0:
+                    reciprocal_columns()
                 neighbour_sums(cb, piece, staged)
                 if cb == 0:
-                    if piece == 0:
-                        reciprocal_columns()
                     spread_r(piece)
                 if cb < PIECEWISE_BLOCKS:
                     place(cb, staged, piece, 1)

@@ -9,7 +9,7 @@ CHANNEL_BLOCKS = C // P
 PIECE = 512
 PIECES = N // PIECE
 BLOCKS_A_PIECE = PIECE // P
-PIECEWISE_BLOCKS = 2
+PLACINGS = ((256, 256, 512), (512, 512), (512, 512), (512, 512))
 
 BF16, F32, U16 = mybir.dt.bfloat16, mybir.dt.float32, mybir.dt.uint16
 MULT = mybir.AluOpType.mult
@@ -26,8 +26,8 @@ def tile_allgnn_kernel(tc, x, w_in, b_in, adj_t, base, offs, out):
         tc.tile_pool(name="h_pool", bufs=2) as h_pool,
         tc.tile_pool(name="staging", bufs=3) as staging,
         tc.psum_pool(name="psum_h", bufs=2) as psum_h,
-        tc.psum_pool(name="psum_r", bufs=1) as psum_r,
-        tc.psum_pool(name="psum_total", bufs=2) as psum_total,
+        tc.psum_pool(name="psum_degree", bufs=1) as psum_degree,
+        tc.psum_pool(name="psum_rows", bufs=3) as psum_rows,
     ):
         offsets = held.tile([P, N // 16], U16, name="offsets")
         nc.sync.dma_start(offsets[:], offs)
@@ -59,8 +59,6 @@ def tile_allgnn_kernel(tc, x, w_in, b_in, adj_t, base, offs, out):
         r_columns = held.tile([P, NODE_BLOCKS], F32, name="r_columns")
         r_rows = held.tile([P, N], F32, name="r_rows")
 
-        BLOCK_EMPTIED_BY_VECTOR = 1
-
         def project(cb):
             h = h_pool.tile([P, N], BF16, name="h")
             for piece in range(PIECES):
@@ -74,10 +72,7 @@ def tile_allgnn_kernel(tc, x, w_in, b_in, adj_t, base, offs, out):
                         stop=(kb == K_BLOCKS - 1),
                     )
                 columns = slice(piece * PIECE, (piece + 1) * PIECE)
-                if cb == BLOCK_EMPTIED_BY_VECTOR:
-                    nc.vector.tensor_scalar_add(h[:, columns], projected[:], bias_columns[:, cb : cb + 1])
-                else:
-                    nc.scalar.activation(h[:, columns], projected[:], IDENTITY, bias=bias_columns[:, cb : cb + 1])
+                nc.scalar.activation(h[:, columns], projected[:], IDENTITY, bias=bias_columns[:, cb : cb + 1])
             return h
 
         def flip(cb, h):
@@ -87,25 +82,22 @@ def tile_allgnn_kernel(tc, x, w_in, b_in, adj_t, base, offs, out):
                 for quarter in range(BLOCKS_A_PIECE):
                     ib = piece * BLOCKS_A_PIECE + quarter
                     nc.tensor.transpose(flipped[:, quarter, :], h[:, ib * P : (ib + 1) * P], identity_bf16[:])
-                if cb == BLOCK_EMPTIED_BY_VECTOR:
-                    nc.vector.tensor_copy(h_flipped[cb][:, blocks, :], flipped[:])
-                else:
-                    nc.scalar.copy(h_flipped[cb][:, blocks, :], flipped[:])
+                nc.scalar.copy(h_flipped[cb][:, blocks, :], flipped[:])
 
-        def neighbour_sums(cb, piece, staged):
-            total = psum_total.tile([P, PIECE], F32, name="total")
+        def neighbour_sums(cb, first, width, staged):
+            total = psum_rows.tile([P, PIECE], F32, name="total", tag="rows")
             for ib in range(NODE_BLOCKS):
                 nc.tensor.matmul(
-                    total[:],
+                    total[:, 0:width],
                     h_flipped[cb][:, ib, :],
-                    adj_blocks[ib][:, piece * PIECE : (piece + 1) * PIECE],
+                    adj_blocks[ib][:, first : first + width],
                     start=(ib == 0),
                     stop=(ib == NODE_BLOCKS - 1),
                 )
-            nc.scalar.copy(staged[:, piece * PIECE : (piece + 1) * PIECE], total[:])
+            nc.scalar.copy(staged[:, first : first + width], total[:, 0:width])
 
         def reciprocal_columns():
-            degree_plus_one = psum_r.tile([P, NODE_BLOCKS], F32, name="degree_plus_one")
+            degree_plus_one = psum_degree.tile([P, NODE_BLOCKS], F32, name="degree_plus_one")
             nc.tensor.matmul(degree_plus_one[:], identity_bf16[:], ones[:], start=True, stop=False)
             for ib in range(NODE_BLOCKS):
                 for jb in range(NODE_BLOCKS):
@@ -119,7 +111,7 @@ def tile_allgnn_kernel(tc, x, w_in, b_in, adj_t, base, offs, out):
             nc.vector.reciprocal(r_columns[:], degree_plus_one[:])
 
         def spread_r(piece):
-            turned = psum_r.tile([P, PIECE], F32, name="turned")
+            turned = psum_rows.tile([P, PIECE], F32, name="turned", tag="rows")
             for quarter in range(BLOCKS_A_PIECE):
                 jb = piece * BLOCKS_A_PIECE + quarter
                 nc.tensor.transpose(
@@ -129,27 +121,28 @@ def tile_allgnn_kernel(tc, x, w_in, b_in, adj_t, base, offs, out):
                 )
             nc.scalar.copy(r_rows[:, piece * PIECE : (piece + 1) * PIECE], turned[:])
 
-        def place(cb, staged, first_piece, pieces):
-            columns = slice(first_piece * PIECE, (first_piece + pieces) * PIECE)
-            entries = offsets[:, first_piece * (PIECE // 16) : (first_piece + pieces) * (PIECE // 16)]
+        def place(cb, staged, first, width):
+            columns = slice(first, first + width)
+            entries = offsets[:, first // 16 : (first + width) // 16]
             nc.vector.tensor_tensor(windows[cb][:].indirect(entries), staged[:, columns], r_rows[:, columns], MULT)
 
-        for cb in range(2):
-            flip(cb, project(cb))
+        h = project(0)
         for cb in range(CHANNEL_BLOCKS):
-            if cb >= 2:
-                flip(cb, h)
-            if 1 <= cb < CHANNEL_BLOCKS - 1:
+            flip(cb, h)
+            if cb == 0:
+                reciprocal_columns()
+            elif cb + 1 < CHANNEL_BLOCKS:
                 h = project(cb + 1)
             staged = staging.tile([P, N], F32, name="staged")
-            for piece in range(PIECES):
-                if cb == 0 and piece == 0:
-                    reciprocal_columns()
-                neighbour_sums(cb, piece, staged)
-                if cb == 0:
-                    spread_r(piece)
-                if cb < PIECEWISE_BLOCKS:
-                    place(cb, staged, piece, 1)
-            if cb >= PIECEWISE_BLOCKS:
-                place(cb, staged, 0, PIECES)
+            first = 0
+            for width in PLACINGS[cb]:
+                for bank_first in range(first, first + width, PIECE):
+                    neighbour_sums(cb, bank_first, min(width, PIECE), staged)
+                if cb == 0 and first == 0:
+                    for piece in range(PIECES):
+                        spread_r(piece)
+                place(cb, staged, first, width)
+                if cb == 0 and first == 0:
+                    h = project(1)
+                first += width
             nc.sync.dma_start(out[cb * P : (cb + 1) * P, :], windows[cb][:])

@@ -9,7 +9,8 @@ CHANNEL_BLOCKS = C // P
 PIECE = 512
 PIECES = N // PIECE
 BLOCKS_A_PIECE = PIECE // P
-PLACINGS = ((256, 256, 512), (512, 512), (512, 512), (512, 512))
+ROWS_A_LOAD = 2 * P
+PLACINGS = ((256, 256, 256, 256), (512, 512), (512, 512), (512, 512))
 
 BF16, F32, U16 = mybir.dt.bfloat16, mybir.dt.float32, mybir.dt.uint16
 MULT = mybir.AluOpType.mult
@@ -25,30 +26,47 @@ def tile_allgnn_kernel(tc, x, w_in, b_in, adj_t, base, offs, out):
         tc.tile_pool(name="held", bufs=1) as held,
         tc.tile_pool(name="h_pool", bufs=2) as h_pool,
         tc.tile_pool(name="staging", bufs=3) as staging,
-        tc.psum_pool(name="psum_h", bufs=2) as psum_h,
+        tc.psum_pool(name="psum_h", bufs=4) as psum_h,
         tc.psum_pool(name="psum_degree", bufs=1) as psum_degree,
         tc.psum_pool(name="psum_rows", bufs=3) as psum_rows,
     ):
-        offsets = held.tile([P, N // 16], U16, name="offsets")
-        nc.sync.dma_start(offsets[:], offs)
-
         w_blocks = [held.tile([P, C], BF16, name=f"w{kb}") for kb in range(K_BLOCKS)]
         x_blocks = [held.tile([P, N], BF16, name=f"x{kb}") for kb in range(K_BLOCKS)]
         for kb in range(K_BLOCKS):
             nc.sync.dma_start(w_blocks[kb][:], w_in[kb * P : (kb + 1) * P, :])
             nc.sync.dma_start(x_blocks[kb][:], x[kb * P : (kb + 1) * P, :])
-        adj_blocks = [held.tile([P, N], BF16, name=f"adj{ib}") for ib in range(NODE_BLOCKS)]
-        for ib in range(NODE_BLOCKS):
-            nc.sync.dma_start(adj_blocks[ib][:], adj_t[ib * P : (ib + 1) * P, :])
+        offsets = held.tile([P, N // 16], U16, name="offsets")
+        nc.sync.dma_start(offsets[:], offs)
+
+        adj_halves = [
+            [held.tile([P, 2, PIECE], BF16, name=f"adj{piece}_{load}") for load in range(N // ROWS_A_LOAD)]
+            for piece in range(PIECES)
+        ]
         windows = [held.tile([P, S], F32, name=f"window{cb}") for cb in range(CHANNEL_BLOCKS)]
-        for cb in range(CHANNEL_BLOCKS):
+
+        def load_adj_half(piece):
+            for load in range(N // ROWS_A_LOAD):
+                rows = adj_t[load * ROWS_A_LOAD : (load + 1) * ROWS_A_LOAD, piece * PIECE : (piece + 1) * PIECE]
+                nc.sync.dma_start(adj_halves[piece][load][:], rows.rearrange("(b p) j -> p b j", p=P))
+
+        def load_window(cb):
             nc.sync.dma_start(windows[cb][:], base[cb * P : (cb + 1) * P, :])
+
+        load_adj_half(0)
+        load_window(0)
+        load_adj_half(1)
+        for cb in range(1, CHANNEL_BLOCKS):
+            load_window(cb)
+
+        def adj_columns(ib, first, width):
+            inside = first % PIECE
+            return adj_halves[first // PIECE][ib // 2][:, ib % 2, inside : inside + width]
 
         bias_columns = held.tile([P, CHANNEL_BLOCKS], F32, name="bias_columns")
         with nc.allow_non_contiguous_dma(reason="512 numbers, one to a partition and column"):
             nc.scalar.dma_start(bias_columns[:], b_in.rearrange("(cb p) one -> p (cb one)", p=P))
 
-        ones = held.tile([P, NODE_BLOCKS], BF16, name="ones")
+        ones = held.tile([P, BLOCKS_A_PIECE], BF16, name="ones")
         nc.gpsimd.memset(ones[:], 1.0)
         identity_bf16 = held.tile([P, P], BF16, name="identity_bf16")
         make_identity(nc, identity_bf16[:])
@@ -62,7 +80,7 @@ def tile_allgnn_kernel(tc, x, w_in, b_in, adj_t, base, offs, out):
         def project(cb):
             h = h_pool.tile([P, N], BF16, name="h")
             for piece in range(PIECES):
-                projected = psum_h.tile([P, PIECE], F32, name="projected")
+                projected = psum_h.tile([P, PIECE], F32, name="projected", tag="h_bank")
                 for kb in range(K_BLOCKS):
                     nc.tensor.matmul(
                         projected[:],
@@ -72,17 +90,23 @@ def tile_allgnn_kernel(tc, x, w_in, b_in, adj_t, base, offs, out):
                         stop=(kb == K_BLOCKS - 1),
                     )
                 columns = slice(piece * PIECE, (piece + 1) * PIECE)
-                nc.scalar.activation(h[:, columns], projected[:], IDENTITY, bias=bias_columns[:, cb : cb + 1])
+                if cb == 1:
+                    nc.vector.tensor_scalar_add(h[:, columns], projected[:], bias_columns[:, cb : cb + 1])
+                else:
+                    nc.scalar.activation(h[:, columns], projected[:], IDENTITY, bias=bias_columns[:, cb : cb + 1])
             return h
 
         def flip(cb, h):
             for piece in range(PIECES):
                 blocks = slice(piece * BLOCKS_A_PIECE, (piece + 1) * BLOCKS_A_PIECE)
-                flipped = psum_h.tile([P, BLOCKS_A_PIECE, P], BF16, name="flipped")
+                flipped = psum_h.tile([P, BLOCKS_A_PIECE, P], BF16, name="flipped", tag="h_bank")
                 for quarter in range(BLOCKS_A_PIECE):
                     ib = piece * BLOCKS_A_PIECE + quarter
                     nc.tensor.transpose(flipped[:, quarter, :], h[:, ib * P : (ib + 1) * P], identity_bf16[:])
-                nc.scalar.copy(h_flipped[cb][:, blocks, :], flipped[:])
+                if cb == 0 and piece == 1:
+                    nc.vector.tensor_copy(h_flipped[cb][:, blocks, :], flipped[:])
+                else:
+                    nc.scalar.copy(h_flipped[cb][:, blocks, :], flipped[:])
 
         def neighbour_sums(cb, first, width, staged):
             total = psum_rows.tile([P, PIECE], F32, name="total", tag="rows")
@@ -90,25 +114,25 @@ def tile_allgnn_kernel(tc, x, w_in, b_in, adj_t, base, offs, out):
                 nc.tensor.matmul(
                     total[:, 0:width],
                     h_flipped[cb][:, ib, :],
-                    adj_blocks[ib][:, first : first + width],
+                    adj_columns(ib, first, width),
                     start=(ib == 0),
                     stop=(ib == NODE_BLOCKS - 1),
                 )
             nc.scalar.copy(staged[:, first : first + width], total[:, 0:width])
 
-        def reciprocal_columns():
-            degree_plus_one = psum_degree.tile([P, NODE_BLOCKS], F32, name="degree_plus_one")
+        def reciprocal_columns(piece):
+            degree_plus_one = psum_degree.tile([P, BLOCKS_A_PIECE], F32, name="degree_plus_one")
             nc.tensor.matmul(degree_plus_one[:], identity_bf16[:], ones[:], start=True, stop=False)
             for ib in range(NODE_BLOCKS):
-                for jb in range(NODE_BLOCKS):
+                for quarter in range(BLOCKS_A_PIECE):
                     nc.tensor.matmul(
-                        degree_plus_one[:, jb : jb + 1],
-                        adj_blocks[ib][:, jb * P : (jb + 1) * P],
+                        degree_plus_one[:, quarter : quarter + 1],
+                        adj_columns(ib, piece * PIECE + quarter * P, P),
                         ones[:, 0:1],
                         start=False,
-                        stop=(ib == NODE_BLOCKS - 1 and jb == NODE_BLOCKS - 1),
+                        stop=(ib == NODE_BLOCKS - 1 and quarter == BLOCKS_A_PIECE - 1),
                     )
-            nc.vector.reciprocal(r_columns[:], degree_plus_one[:])
+            nc.vector.reciprocal(r_columns[:, piece * BLOCKS_A_PIECE : (piece + 1) * BLOCKS_A_PIECE], degree_plus_one[:])
 
         def spread_r(piece):
             turned = psum_rows.tile([P, PIECE], F32, name="turned", tag="rows")
@@ -126,23 +150,24 @@ def tile_allgnn_kernel(tc, x, w_in, b_in, adj_t, base, offs, out):
             entries = offsets[:, first // 16 : (first + width) // 16]
             nc.vector.tensor_tensor(windows[cb][:].indirect(entries), staged[:, columns], r_rows[:, columns], MULT)
 
-        h = project(0)
+        h_of = {0: project(0), 1: project(1)}
+        reciprocal_columns(0)
+        flip(0, h_of[0])
+        spread_r(0)
+
         for cb in range(CHANNEL_BLOCKS):
-            flip(cb, h)
-            if cb == 0:
-                reciprocal_columns()
-            elif cb + 1 < CHANNEL_BLOCKS:
-                h = project(cb + 1)
             staged = staging.tile([P, N], F32, name="staged")
             first = 0
             for width in PLACINGS[cb]:
-                for bank_first in range(first, first + width, PIECE):
-                    neighbour_sums(cb, bank_first, min(width, PIECE), staged)
-                if cb == 0 and first == 0:
-                    for piece in range(PIECES):
-                        spread_r(piece)
+                neighbour_sums(cb, first, width, staged)
+                if cb == 0 and first + width == PIECE:
+                    reciprocal_columns(1)
+                if cb == 0 and first == PIECE:
+                    spread_r(1)
                 place(cb, staged, first, width)
-                if cb == 0 and first == 0:
-                    h = project(1)
+                if first == 0 and cb + 1 < CHANNEL_BLOCKS:
+                    flip(cb + 1, h_of[cb + 1])
                 first += width
+            if cb + 2 < CHANNEL_BLOCKS:
+                h_of[cb + 2] = project(cb + 2)
             nc.sync.dma_start(out[cb * P : (cb + 1) * P, :], windows[cb][:])

@@ -10,7 +10,7 @@ PIECE = 512
 PIECES = N // PIECE
 BLOCKS_A_PIECE = PIECE // P
 ROWS_A_LOAD = 2 * P
-PLACINGS = ((256, 256, 256, 256), (512, 512), (512, 512), (512, 512))
+PLACINGS = ((256, 256, 512), (512, 512), (512, 512), (1024,))
 
 BF16, F32, U16 = mybir.dt.bfloat16, mybir.dt.float32, mybir.dt.uint16
 MULT = mybir.AluOpType.mult
@@ -159,7 +159,8 @@ def tile_allgnn_kernel(tc, x, w_in, b_in, adj_t, base, offs, out):
             staged = staging.tile([P, N], F32, name="staged")
             first = 0
             for width in PLACINGS[cb]:
-                neighbour_sums(cb, first, width, staged)
+                for bank_first in range(first, first + width, PIECE):
+                    neighbour_sums(cb, bank_first, min(width, PIECE), staged)
                 if cb == 0 and first + width == PIECE:
                     reciprocal_columns(1)
                 if cb == 0 and first == PIECE:

@@ -10,7 +10,6 @@ PIECE = 512
 PIECES = N // PIECE
 BLOCKS_A_PIECE = PIECE // P
 ROWS_A_LOAD = 2 * P
-PLACINGS = ((256, 256, 512), (512, 512), (512, 512), (1024,))
 
 BF16, F32, U16 = mybir.dt.bfloat16, mybir.dt.float32, mybir.dt.uint16
 MULT = mybir.AluOpType.mult
@@ -25,7 +24,7 @@ def tile_allgnn_kernel(tc, x, w_in, b_in, adj_t, base, offs, out):
     with (
         tc.tile_pool(name="held", bufs=1) as held,
         tc.tile_pool(name="h_pool", bufs=2) as h_pool,
-        tc.tile_pool(name="staging", bufs=3) as staging,
+        tc.tile_pool(name="staging", bufs=4) as staging,
         tc.psum_pool(name="psum_h", bufs=4) as psum_h,
         tc.psum_pool(name="psum_degree", bufs=1) as psum_degree,
         tc.psum_pool(name="psum_rows", bufs=3) as psum_rows,
@@ -155,20 +154,27 @@ def tile_allgnn_kernel(tc, x, w_in, b_in, adj_t, base, offs, out):
         flip(0, h_of[0])
         spread_r(0)
 
-        for cb in range(CHANNEL_BLOCKS):
-            staged = staging.tile([P, N], F32, name="staged")
-            first = 0
-            for width in PLACINGS[cb]:
-                for bank_first in range(first, first + width, PIECE):
-                    neighbour_sums(cb, bank_first, min(width, PIECE), staged)
-                if cb == 0 and first + width == PIECE:
-                    reciprocal_columns(1)
-                if cb == 0 and first == PIECE:
-                    spread_r(1)
-                place(cb, staged, first, width)
-                if first == 0 and cb + 1 < CHANNEL_BLOCKS:
-                    flip(cb + 1, h_of[cb + 1])
-                first += width
-            if cb + 2 < CHANNEL_BLOCKS:
-                h_of[cb + 2] = project(cb + 2)
-            nc.sync.dma_start(out[cb * P : (cb + 1) * P, :], windows[cb][:])
+        for pair in ((0, 1), (2, 3)):
+            staged_of = {cb: staging.tile([P, N], F32, name="staged") for cb in pair}
+            for piece in range(PIECES):
+                for cb in pair:
+                    first = piece * PIECE
+                    for width in (PIECE // 2, PIECE // 2) if (cb, piece) == (0, 0) else (PIECE,):
+                        neighbour_sums(cb, first, width, staged_of[cb])
+                        if (cb, first) == (1, 0):
+                            reciprocal_columns(1)
+                        if (cb, first) == (0, PIECE):
+                            spread_r(1)
+                        place(cb, staged_of[cb], first, width)
+                        if (cb, first) == (0, 0):
+                            flip(1, h_of[1])
+                        first += width
+                    if (cb, piece) == (1, 0):
+                        h_of[2] = project(2)
+                    if (cb, piece) == (0, 1):
+                        flip(2, h_of[2])
+                        h_of[3] = project(3)
+                    if (cb, piece) == (1, 1):
+                        flip(3, h_of[3])
+                    if piece == PIECES - 1:
+                        nc.sync.dma_start(out[cb * P : (cb + 1) * P, :], windows[cb][:])

@@ -33,7 +33,10 @@ def tile_allgnn_kernel(tc, x, w_in, b_in, adj_t, base, offs, out):
         x_blocks = [held.tile([P, N], BF16, name=f"x{kb}") for kb in range(K_BLOCKS)]
         for kb in range(K_BLOCKS):
             nc.sync.dma_start(w_blocks[kb][:], w_in[kb * P : (kb + 1) * P, :])
-            nc.sync.dma_start(x_blocks[kb][:], x[kb * P : (kb + 1) * P, :])
+        for piece in range(PIECES):
+            columns = slice(piece * PIECE, (piece + 1) * PIECE)
+            for kb in range(K_BLOCKS):
+                nc.sync.dma_start(x_blocks[kb][:, columns], x[kb * P : (kb + 1) * P, columns])
         offsets = held.tile([P, N // 16], U16, name="offsets")
         nc.sync.dma_start(offsets[:], offs)
 
@@ -48,8 +51,11 @@ def tile_allgnn_kernel(tc, x, w_in, b_in, adj_t, base, offs, out):
                 rows = adj_t[load * ROWS_A_LOAD : (load + 1) * ROWS_A_LOAD, piece * PIECE : (piece + 1) * PIECE]
                 nc.sync.dma_start(adj_halves[piece][load][:], rows.rearrange("(b p) j -> p b j", p=P))
 
+        base_blocks = base.rearrange("(p cb) s -> cb p s", cb=CHANNEL_BLOCKS)
+        out_blocks = out.rearrange("(p cb) s -> cb p s", cb=CHANNEL_BLOCKS)
+
         def load_window(cb):
-            nc.sync.dma_start(windows[cb][:], base[cb * P : (cb + 1) * P, :])
+            nc.sync.dma_start(windows[cb][:], base_blocks[cb])
 
         load_adj_half(0)
         load_window(0)
@@ -62,8 +68,7 @@ def tile_allgnn_kernel(tc, x, w_in, b_in, adj_t, base, offs, out):
             return adj_halves[first // PIECE][ib // 2][:, ib % 2, inside : inside + width]
 
         bias_columns = held.tile([P, CHANNEL_BLOCKS], F32, name="bias_columns")
-        with nc.allow_non_contiguous_dma(reason="512 numbers, one to a partition and column"):
-            nc.scalar.dma_start(bias_columns[:], b_in.rearrange("(cb p) one -> p (cb one)", p=P))
+        nc.scalar.dma_start(bias_columns[:], b_in.rearrange("(p cb) one -> p (cb one)", cb=CHANNEL_BLOCKS))
 
         ones = held.tile([P, BLOCKS_A_PIECE], BF16, name="ones")
         nc.gpsimd.memset(ones[:], 1.0)
@@ -83,7 +88,7 @@ def tile_allgnn_kernel(tc, x, w_in, b_in, adj_t, base, offs, out):
                 for kb in range(K_BLOCKS):
                     nc.tensor.matmul(
                         projected[:],
-                        w_blocks[kb][:, cb * P : (cb + 1) * P],
+                        w_blocks[kb][:].rearrange("k (p cb) -> k cb p", cb=CHANNEL_BLOCKS)[:, cb, :],
                         x_blocks[kb][:, piece * PIECE : (piece + 1) * PIECE],
                         start=(kb == 0),
                         stop=(kb == K_BLOCKS - 1),
@@ -177,4 +182,4 @@ def tile_allgnn_kernel(tc, x, w_in, b_in, adj_t, base, offs, out):
                     if (cb, piece) == (1, 1):
                         flip(3, h_of[3])
                     if piece == PIECES - 1:
-                        nc.sync.dma_start(out[cb * P : (cb + 1) * P, :], windows[cb][:])
+                        nc.sync.dma_start(out_blocks[cb], windows[cb][:])

@@ -10,9 +10,10 @@ PIECE = 512
 PIECES = N // PIECE
 BLOCKS_A_PIECE = PIECE // P
 ROWS_A_LOAD = 2 * P
+EARLY_LOADS = 3
 
 BF16, F32, U16 = mybir.dt.bfloat16, mybir.dt.float32, mybir.dt.uint16
-MULT = mybir.AluOpType.mult
+MULT, ADD = mybir.AluOpType.mult, mybir.AluOpType.add
 IDENTITY = mybir.ActivationFunctionType.Identity
 
 FLOPS = 2 * IN * C * N + 2 * C * N * N + N * N
@@ -31,11 +32,11 @@ def tile_allgnn_kernel(tc, x, w_in, b_in, adj_t, base, offs, out):
     ):
         w_blocks = [held.tile([P, C], BF16, name=f"w{kb}") for kb in range(K_BLOCKS)]
         x_blocks = [held.tile([P, N], BF16, name=f"x{kb}") for kb in range(K_BLOCKS)]
-        for kb in range(K_BLOCKS):
-            nc.sync.dma_start(w_blocks[kb][:], w_in[kb * P : (kb + 1) * P, :])
         for piece in range(PIECES):
             columns = slice(piece * PIECE, (piece + 1) * PIECE)
             for kb in range(K_BLOCKS):
+                if piece == 0:
+                    nc.sync.dma_start(w_blocks[kb][:], w_in[kb * P : (kb + 1) * P, :])
                 nc.sync.dma_start(x_blocks[kb][:, columns], x[kb * P : (kb + 1) * P, columns])
         offsets = held.tile([P, N // 16], U16, name="offsets")
         nc.sync.dma_start(offsets[:], offs)
@@ -81,36 +82,39 @@ def tile_allgnn_kernel(tc, x, w_in, b_in, adj_t, base, offs, out):
         r_columns = held.tile([P, NODE_BLOCKS], F32, name="r_columns")
         r_rows = held.tile([P, N], F32, name="r_rows")
 
+        def project_bank(cb, piece, h):
+            columns = slice(piece * PIECE, (piece + 1) * PIECE)
+            projected = psum_h.tile([P, PIECE], F32, name="projected", tag="h_bank")
+            for kb in range(K_BLOCKS):
+                nc.tensor.matmul(
+                    projected[:],
+                    w_blocks[kb][:].rearrange("k (p cb) -> k cb p", cb=CHANNEL_BLOCKS)[:, cb, :],
+                    x_blocks[kb][:, columns],
+                    start=(kb == 0),
+                    stop=(kb == K_BLOCKS - 1),
+                )
+            nc.scalar.activation(h[:, columns], projected[:], IDENTITY, bias=bias_columns[:, cb : cb + 1])
+
+        def flip_bank(cb, piece, h):
+            blocks = slice(piece * BLOCKS_A_PIECE, (piece + 1) * BLOCKS_A_PIECE)
+            flipped = psum_h.tile([P, BLOCKS_A_PIECE, P], BF16, name="flipped", tag="h_bank")
+            for quarter in range(BLOCKS_A_PIECE):
+                ib = piece * BLOCKS_A_PIECE + quarter
+                nc.tensor.transpose(flipped[:, quarter, :], h[:, ib * P : (ib + 1) * P], identity_bf16[:])
+            if cb == 0 and piece == 1:
+                nc.vector.tensor_copy(h_flipped[cb][:, blocks, :], flipped[:])
+            else:
+                nc.scalar.copy(h_flipped[cb][:, blocks, :], flipped[:])
+
         def project(cb):
             h = h_pool.tile([P, N], BF16, name="h")
             for piece in range(PIECES):
-                projected = psum_h.tile([P, PIECE], F32, name="projected", tag="h_bank")
-                for kb in range(K_BLOCKS):
-                    nc.tensor.matmul(
-                        projected[:],
-                        w_blocks[kb][:].rearrange("k (p cb) -> k cb p", cb=CHANNEL_BLOCKS)[:, cb, :],
-                        x_blocks[kb][:, piece * PIECE : (piece + 1) * PIECE],
-                        start=(kb == 0),
-                        stop=(kb == K_BLOCKS - 1),
-                    )
-                columns = slice(piece * PIECE, (piece + 1) * PIECE)
-                if cb == 1:
-                    nc.vector.tensor_scalar_add(h[:, columns], projected[:], bias_columns[:, cb : cb + 1])
-                else:
-                    nc.scalar.activation(h[:, columns], projected[:], IDENTITY, bias=bias_columns[:, cb : cb + 1])
+                project_bank(cb, piece, h)
             return h
 
         def flip(cb, h):
             for piece in range(PIECES):
-                blocks = slice(piece * BLOCKS_A_PIECE, (piece + 1) * BLOCKS_A_PIECE)
-                flipped = psum_h.tile([P, BLOCKS_A_PIECE, P], BF16, name="flipped", tag="h_bank")
-                for quarter in range(BLOCKS_A_PIECE):
-                    ib = piece * BLOCKS_A_PIECE + quarter
-                    nc.tensor.transpose(flipped[:, quarter, :], h[:, ib * P : (ib + 1) * P], identity_bf16[:])
-                if cb == 0 and piece == 1:
-                    nc.vector.tensor_copy(h_flipped[cb][:, blocks, :], flipped[:])
-                else:
-                    nc.scalar.copy(h_flipped[cb][:, blocks, :], flipped[:])
+                flip_bank(cb, piece, h)
 
         def neighbour_sums(cb, first, width, staged):
             total = psum_rows.tile([P, PIECE], F32, name="total", tag="rows")
@@ -124,17 +128,28 @@ def tile_allgnn_kernel(tc, x, w_in, b_in, adj_t, base, offs, out):
                 )
             nc.scalar.copy(staged[:, first : first + width], total[:, 0:width])
 
-        def reciprocal_columns(piece):
+        def add_up_early_loads():
+            pair_sums = []
+            for load in range(EARLY_LOADS):
+                pair_sum = held.tile([P, PIECE], BF16, name=f"pair_sum{load}")
+                nc.vector.tensor_tensor(pair_sum[:], adj_halves[0][load][:, 0, :], adj_halves[0][load][:, 1, :], ADD)
+                pair_sums.append(pair_sum)
+                if load == 1:
+                    four_blocks = held.tile([P, PIECE], BF16, name="four_blocks")
+                    nc.vector.tensor_tensor(four_blocks[:], pair_sums[0][:], pair_sums[1][:], ADD)
+            return [four_blocks[:], pair_sums[2][:]]
+
+        def reciprocal_columns(piece, row_blocks):
             degree_plus_one = psum_degree.tile([P, BLOCKS_A_PIECE], F32, name="degree_plus_one")
             nc.tensor.matmul(degree_plus_one[:], identity_bf16[:], ones[:], start=True, stop=False)
-            for ib in range(NODE_BLOCKS):
+            for number, row_block in enumerate(row_blocks):
                 for quarter in range(BLOCKS_A_PIECE):
                     nc.tensor.matmul(
                         degree_plus_one[:, quarter : quarter + 1],
-                        adj_columns(ib, piece * PIECE + quarter * P, P),
+                        row_block[:, quarter * P : (quarter + 1) * P],
                         ones[:, 0:1],
                         start=False,
-                        stop=(ib == NODE_BLOCKS - 1 and quarter == BLOCKS_A_PIECE - 1),
+                        stop=(number == len(row_blocks) - 1 and quarter == BLOCKS_A_PIECE - 1),
                     )
             nc.vector.reciprocal(r_columns[:, piece * BLOCKS_A_PIECE : (piece + 1) * BLOCKS_A_PIECE], degree_plus_one[:])
 
@@ -154,9 +169,13 @@ def tile_allgnn_kernel(tc, x, w_in, b_in, adj_t, base, offs, out):
             entries = offsets[:, first // 16 : (first + width) // 16]
             nc.vector.tensor_tensor(windows[cb][:].indirect(entries), staged[:, columns], r_rows[:, columns], MULT)
 
-        h_of = {0: project(0), 1: project(1)}
-        reciprocal_columns(0)
-        flip(0, h_of[0])
+        summed_blocks = add_up_early_loads()
+        h_of = {0: project(0), 1: h_pool.tile([P, N], BF16, name="h")}
+        flip_bank(0, 0, h_of[0])
+        project_bank(1, 0, h_of[1])
+        flip_bank(0, 1, h_of[0])
+        reciprocal_columns(0, summed_blocks + [adj_columns(ib, 0, PIECE) for ib in range(2 * EARLY_LOADS, NODE_BLOCKS)])
+        project_bank(1, 1, h_of[1])
         spread_r(0)
 
         for pair in ((0, 1), (2, 3)):
@@ -167,7 +186,7 @@ def tile_allgnn_kernel(tc, x, w_in, b_in, adj_t, base, offs, out):
                     for width in (PIECE // 2, PIECE // 2) if (cb, piece) == (0, 0) else (PIECE,):
                         neighbour_sums(cb, first, width, staged_of[cb])
                         if (cb, first) == (1, 0):
-                            reciprocal_columns(1)
+                            reciprocal_columns(1, [adj_columns(ib, PIECE, PIECE) for ib in range(NODE_BLOCKS)])
                         if (cb, first) == (0, PIECE):
                             spread_r(1)
                         place(cb, staged_of[cb], first, width)

@@ -178,27 +178,38 @@ def tile_allgnn_kernel(tc, x, w_in, b_in, adj_t, base, offs, out):
         project_bank(1, 1, h_of[1])
         spread_r(0)
 
-        for pair in ((0, 1), (2, 3)):
-            staged_of = {cb: staging.tile([P, N], F32, name="staged") for cb in pair}
-            for piece in range(PIECES):
-                for cb in pair:
-                    first = piece * PIECE
-                    for width in (PIECE // 2, PIECE // 2) if (cb, piece) == (0, 0) else (PIECE,):
-                        neighbour_sums(cb, first, width, staged_of[cb])
-                        if (cb, first) == (1, 0):
-                            reciprocal_columns(1, [adj_columns(ib, PIECE, PIECE) for ib in range(NODE_BLOCKS)])
-                        if (cb, first) == (0, PIECE):
-                            spread_r(1)
-                        place(cb, staged_of[cb], first, width)
-                        if (cb, first) == (0, 0):
-                            flip(1, h_of[1])
-                        first += width
-                    if (cb, piece) == (1, 0):
-                        h_of[2] = project(2)
-                    if (cb, piece) == (0, 1):
-                        flip(2, h_of[2])
-                        h_of[3] = project(3)
-                    if (cb, piece) == (1, 1):
-                        flip(3, h_of[3])
-                    if piece == PIECES - 1:
-                        nc.sync.dma_start(out_blocks[cb], windows[cb][:])
+        staged_of = {cb: staging.tile([P, N], F32, name="staged") for cb in range(CHANNEL_BLOCKS)}
+
+        def sum_and_place(cb, first, width):
+            neighbour_sums(cb, first, width, staged_of[cb])
+            place(cb, staged_of[cb], first, width)
+
+        def store(cb):
+            nc.sync.dma_start(out_blocks[cb], windows[cb][:])
+
+        sum_and_place(0, 0, PIECE // 2)
+        flip(1, h_of[1])
+        sum_and_place(0, PIECE // 2, PIECE // 2)
+        neighbour_sums(1, 0, PIECE, staged_of[1])
+        reciprocal_columns(1, [adj_columns(ib, PIECE, PIECE) for ib in range(NODE_BLOCKS)])
+        place(1, staged_of[1], 0, PIECE)
+        neighbour_sums(0, PIECE, PIECE, staged_of[0])
+        spread_r(1)
+        place(0, staged_of[0], PIECE, PIECE)
+        store(0)
+        sum_and_place(1, PIECE, PIECE)
+        store(1)
+
+        h_of[2] = project(2)
+        h_of[3] = h_pool.tile([P, N], BF16, name="h")
+        flip_bank(2, 0, h_of[2])
+        project_bank(3, 0, h_of[3])
+        flip_bank(2, 1, h_of[2])
+        sum_and_place(2, 0, PIECE)
+        project_bank(3, 1, h_of[3])
+        flip(3, h_of[3])
+        sum_and_place(2, PIECE, PIECE)
+        store(2)
+        for piece in range(PIECES):
+            sum_and_place(3, piece * PIECE, PIECE)
+        store(3)

@@ -197,19 +197,18 @@ def tile_allgnn_kernel(tc, x, w_in, b_in, adj_t, base, offs, out):
         spread_r(1)
         place(0, staged_of[0], PIECE, PIECE)
         store(0)
+        h_of[2] = project(2)
         sum_and_place(1, PIECE, PIECE)
         store(1)
-
-        h_of[2] = project(2)
+        flip(2, h_of[2])
         h_of[3] = h_pool.tile([P, N], BF16, name="h")
-        flip_bank(2, 0, h_of[2])
         project_bank(3, 0, h_of[3])
-        flip_bank(2, 1, h_of[2])
         sum_and_place(2, 0, PIECE)
         project_bank(3, 1, h_of[3])
-        flip(3, h_of[3])
+        flip_bank(3, 0, h_of[3])
         sum_and_place(2, PIECE, PIECE)
         store(2)
+        flip_bank(3, 1, h_of[3])
         for piece in range(PIECES):
             sum_and_place(3, piece * PIECE, PIECE)
         store(3)

@@ -201,14 +201,10 @@ def tile_allgnn_kernel(tc, x, w_in, b_in, adj_t, base, offs, out):
         sum_and_place(1, PIECE, PIECE)
         store(1)
         flip(2, h_of[2])
-        h_of[3] = h_pool.tile([P, N], BF16, name="h")
-        project_bank(3, 0, h_of[3])
+        h_of[3] = project(3)
         sum_and_place(2, 0, PIECE)
-        project_bank(3, 1, h_of[3])
-        flip_bank(3, 0, h_of[3])
-        sum_and_place(2, PIECE, PIECE)
-        store(2)
-        flip_bank(3, 1, h_of[3])
-        for piece in range(PIECES):
-            sum_and_place(3, piece * PIECE, PIECE)
-        store(3)
+        flip(3, h_of[3])
+        sum_and_place(3, 0, PIECE)
+        for cb in (2, 3):
+            sum_and_place(cb, PIECE, PIECE)
+            store(cb)

@@ -126,7 +126,10 @@ def tile_allgnn_kernel(tc, x, w_in, b_in, adj_t, base, offs, out):
                     start=(ib == 0),
                     stop=(ib == NODE_BLOCKS - 1),
                 )
-            nc.scalar.copy(staged[:, first : first + width], total[:, 0:width])
+            if (cb, first) == (0, 0):
+                nc.vector.tensor_copy(staged[:, first : first + width], total[:, 0:width])
+            else:
+                nc.scalar.copy(staged[:, first : first + width], total[:, 0:width])
 
         def add_up_early_loads():
             pair_sums = []

import concourse.mybir as mybir
from concourse.masks import make_identity

P = 128
IN, C, N, S = 256, 512, 1024, 2048
K_BLOCKS = IN // P
NODE_BLOCKS = N // P
CHANNEL_BLOCKS = C // P
PIECE = 512
PIECES = N // PIECE
BLOCKS_A_PIECE = PIECE // P
ROWS_A_LOAD = 2 * P
EARLY_LOADS = 3

BF16, F32, U16 = mybir.dt.bfloat16, mybir.dt.float32, mybir.dt.uint16
MULT, ADD = mybir.AluOpType.mult, mybir.AluOpType.add
IDENTITY = mybir.ActivationFunctionType.Identity

FLOPS = 2 * IN * C * N + 2 * C * N * N + N * N
BYTES = 2 * (IN * N + IN * C + N * N + N) + 4 * C + 4 * C * (S - N) + 4 * C * S


def tile_allgnn_kernel(tc, x, w_in, b_in, adj_t, base, offs, out):
    nc = tc.nc
    with (
        tc.tile_pool(name="held", bufs=1) as held,
        tc.tile_pool(name="h_pool", bufs=2) as h_pool,
        tc.tile_pool(name="staging", bufs=4) as staging,
        tc.psum_pool(name="psum_h", bufs=4) as psum_h,
        tc.psum_pool(name="psum_degree", bufs=1) as psum_degree,
        tc.psum_pool(name="psum_rows", bufs=3) as psum_rows,
    ):
        w_blocks = [held.tile([P, C], BF16, name=f"w{kb}") for kb in range(K_BLOCKS)]
        x_blocks = [held.tile([P, N], BF16, name=f"x{kb}") for kb in range(K_BLOCKS)]
        for piece in range(PIECES):
            columns = slice(piece * PIECE, (piece + 1) * PIECE)
            for kb in range(K_BLOCKS):
                if piece == 0:
                    nc.sync.dma_start(w_blocks[kb][:], w_in[kb * P : (kb + 1) * P, :])
                nc.sync.dma_start(x_blocks[kb][:, columns], x[kb * P : (kb + 1) * P, columns])
        offsets = held.tile([P, N // 16], U16, name="offsets")
        nc.sync.dma_start(offsets[:], offs)

        adj_halves = [
            [held.tile([P, 2, PIECE], BF16, name=f"adj{piece}_{load}") for load in range(N // ROWS_A_LOAD)]
            for piece in range(PIECES)
        ]
        windows = [held.tile([P, S], F32, name=f"window{cb}") for cb in range(CHANNEL_BLOCKS)]

        def load_adj_half(piece):
            for load in range(N // ROWS_A_LOAD):
                rows = adj_t[load * ROWS_A_LOAD : (load + 1) * ROWS_A_LOAD, piece * PIECE : (piece + 1) * PIECE]
                nc.sync.dma_start(adj_halves[piece][load][:], rows.rearrange("(b p) j -> p b j", p=P))

        base_blocks = base.rearrange("(p cb) s -> cb p s", cb=CHANNEL_BLOCKS)
        out_blocks = out.rearrange("(p cb) s -> cb p s", cb=CHANNEL_BLOCKS)

        def load_window(cb):
            nc.sync.dma_start(windows[cb][:], base_blocks[cb])

        load_adj_half(0)
        load_window(0)
        load_adj_half(1)
        for cb in range(1, CHANNEL_BLOCKS):
            load_window(cb)

        def adj_columns(ib, first, width):
            inside = first % PIECE
            return adj_halves[first // PIECE][ib // 2][:, ib % 2, inside : inside + width]

        bias_columns = held.tile([P, CHANNEL_BLOCKS], F32, name="bias_columns")
        nc.scalar.dma_start(bias_columns[:], b_in.rearrange("(p cb) one -> p (cb one)", cb=CHANNEL_BLOCKS))

        ones = held.tile([P, BLOCKS_A_PIECE], BF16, name="ones")
        nc.gpsimd.memset(ones[:], 1.0)
        identity_bf16 = held.tile([P, P], BF16, name="identity_bf16")
        make_identity(nc, identity_bf16[:])
        identity_f32 = held.tile([P, P], F32, name="identity_f32")
        make_identity(nc, identity_f32[:])

        h_flipped = [held.tile([P, NODE_BLOCKS, P], BF16, name=f"h_flipped{cb}") for cb in range(CHANNEL_BLOCKS)]
        r_columns = held.tile([P, NODE_BLOCKS], F32, name="r_columns")
        r_rows = held.tile([P, N], F32, name="r_rows")

        def project_bank(cb, piece, h):
            columns = slice(piece * PIECE, (piece + 1) * PIECE)
            projected = psum_h.tile([P, PIECE], F32, name="projected", tag="h_bank")
            for kb in range(K_BLOCKS):
                nc.tensor.matmul(
                    projected[:],
                    w_blocks[kb][:].rearrange("k (p cb) -> k cb p", cb=CHANNEL_BLOCKS)[:, cb, :],
                    x_blocks[kb][:, columns],
                    start=(kb == 0),
                    stop=(kb == K_BLOCKS - 1),
                )
            nc.scalar.activation(h[:, columns], projected[:], IDENTITY, bias=bias_columns[:, cb : cb + 1])

        def flip_bank(cb, piece, h):
            blocks = slice(piece * BLOCKS_A_PIECE, (piece + 1) * BLOCKS_A_PIECE)
            flipped = psum_h.tile([P, BLOCKS_A_PIECE, P], BF16, name="flipped", tag="h_bank")
            for quarter in range(BLOCKS_A_PIECE):
                ib = piece * BLOCKS_A_PIECE + quarter
                nc.tensor.transpose(flipped[:, quarter, :], h[:, ib * P : (ib + 1) * P], identity_bf16[:])
            if cb == 0 and piece == 1:
                nc.vector.tensor_copy(h_flipped[cb][:, blocks, :], flipped[:])
            else:
                nc.scalar.copy(h_flipped[cb][:, blocks, :], flipped[:])

        def project(cb):
            h = h_pool.tile([P, N], BF16, name="h")
            for piece in range(PIECES):
                project_bank(cb, piece, h)
            return h

        def flip(cb, h):
            for piece in range(PIECES):
                flip_bank(cb, piece, h)

        def neighbour_sums(cb, first, width, staged):
            total = psum_rows.tile([P, PIECE], F32, name="total", tag="rows")
            for ib in range(NODE_BLOCKS):
                nc.tensor.matmul(
                    total[:, 0:width],
                    h_flipped[cb][:, ib, :],
                    adj_columns(ib, first, width),
                    start=(ib == 0),
                    stop=(ib == NODE_BLOCKS - 1),
                )
            if (cb, first) == (0, 0):
                nc.vector.tensor_copy(staged[:, first : first + width], total[:, 0:width])
            else:
                nc.scalar.copy(staged[:, first : first + width], total[:, 0:width])

        def add_up_early_loads():
            pair_sums = []
            for load in range(EARLY_LOADS):
                pair_sum = held.tile([P, PIECE], BF16, name=f"pair_sum{load}")
                nc.vector.tensor_tensor(pair_sum[:], adj_halves[0][load][:, 0, :], adj_halves[0][load][:, 1, :], ADD)
                pair_sums.append(pair_sum)
                if load == 1:
                    four_blocks = held.tile([P, PIECE], BF16, name="four_blocks")
                    nc.vector.tensor_tensor(four_blocks[:], pair_sums[0][:], pair_sums[1][:], ADD)
            return [four_blocks[:], pair_sums[2][:]]

        def reciprocal_columns(piece, row_blocks):
            degree_plus_one = psum_degree.tile([P, BLOCKS_A_PIECE], F32, name="degree_plus_one")
            nc.tensor.matmul(degree_plus_one[:], identity_bf16[:], ones[:], start=True, stop=False)
            for number, row_block in enumerate(row_blocks):
                for quarter in range(BLOCKS_A_PIECE):
                    nc.tensor.matmul(
                        degree_plus_one[:, quarter : quarter + 1],
                        row_block[:, quarter * P : (quarter + 1) * P],
                        ones[:, 0:1],
                        start=False,
                        stop=(number == len(row_blocks) - 1 and quarter == BLOCKS_A_PIECE - 1),
                    )
            nc.vector.reciprocal(r_columns[:, piece * BLOCKS_A_PIECE : (piece + 1) * BLOCKS_A_PIECE], degree_plus_one[:])

        def spread_r(piece):
            turned = psum_rows.tile([P, PIECE], F32, name="turned", tag="rows")
            for quarter in range(BLOCKS_A_PIECE):
                jb = piece * BLOCKS_A_PIECE + quarter
                nc.tensor.transpose(
                    turned[:, quarter * P : (quarter + 1) * P],
                    r_columns[:, jb : jb + 1].to_broadcast([P, P]),
                    identity_f32[:],
                )
            nc.scalar.copy(r_rows[:, piece * PIECE : (piece + 1) * PIECE], turned[:])

        def place(cb, staged, first, width):
            columns = slice(first, first + width)
            entries = offsets[:, first // 16 : (first + width) // 16]
            nc.vector.tensor_tensor(windows[cb][:].indirect(entries), staged[:, columns], r_rows[:, columns], MULT)

        summed_blocks = add_up_early_loads()
        h_of = {0: project(0), 1: h_pool.tile([P, N], BF16, name="h")}
        flip_bank(0, 0, h_of[0])
        project_bank(1, 0, h_of[1])
        flip_bank(0, 1, h_of[0])
        reciprocal_columns(0, summed_blocks + [adj_columns(ib, 0, PIECE) for ib in range(2 * EARLY_LOADS, NODE_BLOCKS)])
        project_bank(1, 1, h_of[1])
        spread_r(0)

        staged_of = {cb: staging.tile([P, N], F32, name="staged") for cb in range(CHANNEL_BLOCKS)}

        def sum_and_place(cb, first, width):
            neighbour_sums(cb, first, width, staged_of[cb])
            place(cb, staged_of[cb], first, width)

        def store(cb):
            nc.sync.dma_start(out_blocks[cb], windows[cb][:])

        sum_and_place(0, 0, PIECE // 2)
        flip(1, h_of[1])
        sum_and_place(0, PIECE // 2, PIECE // 2)
        neighbour_sums(1, 0, PIECE, staged_of[1])
        reciprocal_columns(1, [adj_columns(ib, PIECE, PIECE) for ib in range(NODE_BLOCKS)])
        place(1, staged_of[1], 0, PIECE)
        neighbour_sums(0, PIECE, PIECE, staged_of[0])
        spread_r(1)
        place(0, staged_of[0], PIECE, PIECE)
        store(0)
        h_of[2] = project(2)
        sum_and_place(1, PIECE, PIECE)
        store(1)
        flip(2, h_of[2])
        h_of[3] = project(3)
        sum_and_place(2, 0, PIECE)
        flip(3, h_of[3])
        sum_and_place(3, 0, PIECE)
        for cb in (2, 3):
            sum_and_place(cb, PIECE, PIECE)
            store(cb)
